import numpy as np
import ml_dtypes


def mxq(x, axis, fmt="e4m3"):
    dtype, down = {"e4m3": (ml_dtypes.float8_e4m3fn, 7), "e5m2": (ml_dtypes.float8_e5m2, 14)}[fmt]
    v = np.moveaxis(np.asarray(x, np.float32).astype(ml_dtypes.bfloat16).astype(np.float64), axis, -1)
    blocks = v.reshape(v.shape[:-1] + (-1, 32))
    amax = np.abs(blocks).max(-1, keepdims=True)
    byte = np.maximum(np.where(amax > 0, np.frexp(amax)[1] - 1 + 127, 0) - down, 1)
    scale = np.exp2(byte - 127.0)
    codes = (blocks / scale).astype(np.float32).astype(dtype).astype(np.float64)
    return np.moveaxis((codes * scale).reshape(v.shape), -1, axis)


WIDE = False


def mx_kscale(k):
    if not WIDE:
        return np.ones(k)
    levels = np.array([10, -10, 5, -5, 0])
    a = np.random.permutation(np.resize(levels, k // 512 * 4)).reshape(k // 512, 4)
    idx = np.arange(k)
    return np.exp2(a[idx // 512, idx % 128 // 32])


BF16 = ml_dtypes.bfloat16


def bf(x):
    return np.asarray(x, np.float32).astype(BF16)


def f64(x):
    return np.asarray(x).astype(np.float64)


B, S, HID, H, KV, D = 1, 512, 2048, 16, 4, 128
EPS = 1e-6
THETA = 10000.0
HALF = D // 2


def rotate_half(x):
    return np.concatenate([-x[..., HALF:], x[..., :HALF]], axis=-1)


def rms_norm(x, w=None):
    n = x * (1.0 / np.sqrt(np.mean(x * x, axis=-1, keepdims=True) + EPS))
    return n if w is None else n * w


def setup_inputs():
    s = mx_kscale(HID)
    c = 0.004 / np.sqrt(HID)
    inv_freq = 1.0 / THETA ** (np.arange(0, D, 2) / D)
    pos = np.random.randint(0, S) + np.arange(S)
    freqs = pos[:, None] * inv_freq[None, :]
    emb = np.concatenate([freqs, freqs], axis=-1)
    return {"hidden_states": bf(np.random.standard_normal((B, S, HID)) * s),
            "cos": bf(np.cos(emb)[None]),
            "sin": bf(np.sin(emb)[None]),
            "Wq": bf(np.random.standard_normal((H * D, HID)) * c / s[None, :]),
            "Wk": bf(np.random.standard_normal((KV * D, HID)) * c / s[None, :]),
            "Wv": bf(np.random.standard_normal((KV * D, HID)) * c / s[None, :]),
            "q_norm_w": bf(0.5 + 0.1 * np.random.standard_normal(D)),
            "k_norm_w": bf(0.5 + 0.1 * np.random.standard_normal(D))}


def reference(hidden_states, cos, sin, Wq, Wk, Wv, q_norm_w, k_norm_w):
    xq = mxq(f64(hidden_states), 2, "e4m3")
    cs = f64(cos)[:, :, None, :]
    sn = f64(sin)[:, :, None, :]
    q = (xq @ mxq(f64(Wq).T, 0, "e4m3")).reshape(B, S, H, D)
    k = (xq @ mxq(f64(Wk).T, 0, "e4m3")).reshape(B, S, KV, D)
    v = (xq @ mxq(f64(Wv).T, 0, "e4m3")).reshape(B, S, KV, D)
    q = rms_norm(q, f64(q_norm_w))
    q = q * cs + rotate_half(q) * sn
    k = rms_norm(k, f64(k_norm_w))
    k = k * cs + rotate_half(k) * sn
    v = rms_norm(v)
    return q.transpose(0, 2, 1, 3), k.transpose(0, 2, 1, 3), v.transpose(0, 2, 1, 3)

@@ -1,0 +1,255 @@
+from contextlib import ExitStack
+
+import concourse.mybir as mybir
+from concourse.masks import make_identity
+
+F32 = mybir.dt.float32
+BF16 = mybir.dt.bfloat16
+U32 = mybir.dt.uint32
+U8 = mybir.dt.uint8
+FP8X4 = mybir.dt.float8_e4m3fn_x4
+ACT = mybir.ActivationFunctionType
+ALU = mybir.AluOpType
+
+P = 128
+TOKENS = 512
+HID = 2048
+D = 128
+HALF = D // 2
+EPS = 1e-6
+BLOCK_ROWS = 512
+ROW_TILES = BLOCK_ROWS // P
+PASSES = HID // 512
+STEP_K = HID // 2
+STEP_PASSES = STEP_K // 512
+PASS_WORDS = 256
+W_BLOCKS = 6
+PREP_STEPS = 2 * (W_BLOCKS + 1)
+MX_STEPS = 2 * W_BLOCKS
+LAG = 4
+
+FLOPS = 2 * TOKENS * HID * (W_BLOCKS * BLOCK_ROWS)
+
+
+def tile_refattention_pa_kernel(
+    tc, hidden_states, cos, sin, Wq, Wk, Wv, q_norm_w, k_norm_w, out_0, out_1, out_2
+):
+    nc = tc.nc
+    with ExitStack() as ctx:
+        const = ctx.enter_context(tc.tile_pool(name="const", bufs=1))
+        raw_pool = ctx.enter_context(tc.tile_pool(name="raw", bufs=1))
+        grouped_pool = ctx.enter_context(tc.tile_pool(name="grouped", bufs=4))
+        words_pool = ctx.enter_context(tc.tile_pool(name="words", bufs=3))
+        small = ctx.enter_context(tc.tile_pool(name="small", bufs=4))
+        work = ctx.enter_context(tc.tile_pool(name="work", bufs=3))
+        stage_pool = ctx.enter_context(tc.tile_pool(name="stage", bufs=2))
+        flip_psum = ctx.enter_context(tc.psum_pool(name="flip", bufs=4))
+        acc_psum = ctx.enter_context(tc.psum_pool(name="acc", bufs=4))
+        ctx.enter_context(tc.manual_schedule())
+
+        gains_row = const.tile([P, 2 * D], BF16, name="gains_row")
+        nc.vector.memset(gains_row[:], 0.0)
+        nc.scalar.dma_start(out=gains_row[0:1, 0:D], in_=q_norm_w.rearrange("(o d) -> o d", o=1))
+        nc.scalar.dma_start(out=gains_row[0:1, D : 2 * D], in_=k_norm_w.rearrange("(o d) -> o d", o=1))
+        cos_sb = const.tile([P, ROW_TILES, D], BF16, name="cos_sb")
+        sin_sb = const.tile([P, ROW_TILES, D], BF16, name="sin_sb")
+        nc.scalar.dma_start(
+            out=cos_sb[:], in_=cos.flatten_outer_dims().rearrange("(p t) d -> p t d", t=ROW_TILES)
+        )
+        nc.scalar.dma_start(
+            out=sin_sb[:], in_=sin.flatten_outer_dims().rearrange("(p t) d -> p t d", t=ROW_TILES)
+        )
+
+        x_rows = hidden_states.flatten_outer_dims().rearrange("(p t) k -> p t k", t=ROW_TILES)
+        row_views = [x_rows]
+        for j in range(4):
+            rows = Wq[j * BLOCK_ROWS : (j + 1) * BLOCK_ROWS, :]
+            row_views.append(rows.rearrange("(r p) k -> p r k", p=P))
+        row_views.append(Wk.rearrange("(r p) k -> p r k", p=P))
+        row_views.append(Wv.rearrange("(r p) k -> p r k", p=P))
+        raw = []
+        for s in range(PREP_STEPS):
+            block, k_half = divmod(s, 2)
+            raw_tile = raw_pool.tile([P, ROW_TILES, STEP_K], BF16, name="raw%d" % s)
+            nc.sync.dma_start(
+                out=raw_tile[:],
+                in_=row_views[block][:, :, k_half * STEP_K : (k_half + 1) * STEP_K],
+            )
+            raw.append(raw_tile)
+
+        ident = const.tile([P, P], F32, name="ident")
+        make_identity(nc, ident[:])
+        ones = const.tile([P, P], BF16, name="ones")
+        nc.vector.memset(ones[:], 1.0)
+        eps_col = const.tile([P, 1], F32, name="eps_col")
+        nc.vector.memset(eps_col[:], EPS)
+        table_warm = const.tile([P, 1], F32, name="table_warm")
+        nc.scalar.activation(out=table_warm[:], in_=eps_col[:], func=ACT.Sqrt)
+
+        gains_ps = flip_psum.tile([P, 2 * D], F32, tag="flip", name="gains_ps")
+        nc.tensor.matmul(out=gains_ps[:], lhsT=ones[:], rhs=gains_row[:], start=True, stop=True)
+        gains = const.tile([P, 2 * D], F32, name="gains")
+        minus_gains = const.tile([P, 2 * D], F32, name="minus_gains")
+        nc.scalar.copy(out=gains[:], in_=gains_ps[:])
+        nc.scalar.mul(out=minus_gains[:], in_=gains_ps[:], mul=-1.0)
+
+        rope = []
+        for which in range(2):
+            first = which * D
+            table = const.tile([P, ROW_TILES, 2, D], F32, name="rope%d" % which)
+            nc.gpsimd.tensor_tensor(
+                out=table[:, :, 0, :],
+                in0=cos_sb[:],
+                in1=gains[:, first : first + D].unsqueeze(1).to_broadcast([P, ROW_TILES, D]),
+                op=ALU.mult,
+            )
+            nc.gpsimd.tensor_tensor(
+                out=table[:, :, 1, 0:HALF],
+                in0=sin_sb[:, :, HALF:D],
+                in1=gains[:, first : first + HALF].unsqueeze(1).to_broadcast([P, ROW_TILES, HALF]),
+                op=ALU.mult,
+            )
+            nc.gpsimd.tensor_tensor(
+                out=table[:, :, 1, HALF:D],
+                in0=sin_sb[:, :, 0:HALF],
+                in1=minus_gains[:, first + HALF : first + D]
+                .unsqueeze(1)
+                .to_broadcast([P, ROW_TILES, HALF]),
+                op=ALU.mult,
+            )
+            rope.append(table)
+
+        out_views = [
+            out_0.rearrange("o h (p t) d -> p (o h) (t d)", t=ROW_TILES),
+            out_1.rearrange("o h (p t) d -> p (o h) (t d)", t=ROW_TILES),
+            out_2.rearrange("o h (p t) d -> p (o h) (t d)", t=ROW_TILES),
+        ]
+
+        codes = {}
+        scales = {}
+        accs = {}
+        stages = {}
+
+        def transpose_step(s):
+            words = raw[s][:].bitcast(F32)
+            banks = []
+            for local_pass in range(STEP_PASSES):
+                for pair in range(2):
+                    bank = flip_psum.tile([P, 2, 2 * P], F32, tag="flip", name="bank")
+                    for r in range(2):
+                        for u in range(2):
+                            first = local_pass * PASS_WORDS + u * P
+                            nc.tensor.transpose(
+                                bank[:, u, r * P : (r + 1) * P],
+                                words[:, 2 * pair + r, first : first + P],
+                                ident[:],
+                            )
+                    banks.append(bank)
+            return banks
+
+        def regroup_and_quantise(s, local_pass, banks):
+            block, k_half = divmod(s, 2)
+            if k_half == 0 and local_pass == 0:
+                pool = const if block == 0 else words_pool
+                codes[block] = pool.tile([P, PASSES, BLOCK_ROWS], U32, align_bytes=64, name="codes")
+                scales[block] = pool.tile([P, PASSES, BLOCK_ROWS], U8, align_bytes=64, name="scales")
+            grouped = grouped_pool.tile([P, 4 * BLOCK_ROWS], BF16, align_bytes=64, name="grouped")
+            grouped_words = grouped[:].bitcast(F32)
+            for pair in range(2):
+                engine_copy = nc.vector.tensor_copy if (s <= LAG and pair == 1) else nc.scalar.copy
+                engine_copy(
+                    out=grouped_words[:, pair * 4 * P : (pair + 1) * 4 * P].rearrange(
+                        "p (c u) -> p c u", u=2
+                    ),
+                    in_=banks[pair][:].rearrange("p u c -> p c u"),
+                )
+            g = k_half * STEP_PASSES + local_pass
+            nc.vector.quantize_mx(
+                out=codes[block][:, g, :].bitcast(FP8X4),
+                scales=scales[block][:, g, :],
+                in_=grouped[:],
+            )
+
+        def matmul_step(m):
+            w_block, tile_pair = divmod(m, 2)
+            for i in range(2):
+                t = 2 * tile_pair + i
+                acc = acc_psum.tile([P, BLOCK_ROWS], F32, tag="acc", name="acc")
+                for g in range(PASSES):
+                    nc.tensor.matmul_mx(
+                        out=acc[:],
+                        lhsT=codes[0][:, g, t * P : (t + 1) * P].bitcast(FP8X4),
+                        lhsT_scale=scales[0][:, g, t * P : (t + 1) * P],
+                        rhs=codes[w_block + 1][:, g, :].bitcast(FP8X4),
+                        rhs_scale=scales[w_block + 1][:, g, :],
+                        start=(g == 0),
+                        stop=(g == PASSES - 1),
+                    )
+                accs[(w_block, t)] = acc
+
+        def norm_and_rope(w_block, t):
+            acc = accs[(w_block, t)]
+            if t == 0:
+                stages[w_block] = stage_pool.tile([P, ROW_TILES, ROW_TILES, D], F32, name="stage")
+            stage = stages[w_block]
+            squares = work.tile([P, BLOCK_ROWS], F32, name="squares")
+            sum_sq = small.tile([P, ROW_TILES], F32, name="sum_sq")
+            for h in range(ROW_TILES):
+                nc.scalar.activation(
+                    out=squares[:, h * D : (h + 1) * D],
+                    in_=acc[:, h * D : (h + 1) * D],
+                    func=ACT.Square,
+                    accum_out=sum_sq[:, h : h + 1],
+                )
+            rms = small.tile([P, ROW_TILES], F32, name="rms")
+            nc.scalar.activation(out=rms[:], in_=sum_sq[:], func=ACT.Sqrt, bias=eps_col[:], scale=1.0 / D)
+            inv_rms = small.tile([P, ROW_TILES], F32, name="inv_rms")
+            nc.vector.reciprocal(out=inv_rms[:], in_=rms[:])
+            if w_block == W_BLOCKS - 1:
+                nc.vector.tensor_tensor(
+                    out=stage[:, :, t, :],
+                    in0=acc[:].rearrange("p (h d) -> p h d", d=D),
+                    in1=inv_rms[:].unsqueeze(2).to_broadcast([P, ROW_TILES, D]),
+                    op=ALU.mult,
+                )
+            else:
+                table = rope[0] if w_block < 4 else rope[1]
+                terms = work.tile([P, ROW_TILES, 2, D], F32, name="terms")
+                for h in range(ROW_TILES):
+                    nc.vector.scalar_tensor_tensor(
+                        out=terms[:, h, :, :],
+                        in0=acc[:, h * D : (h + 1) * D].unsqueeze(1).to_broadcast([P, 2, D]),
+                        scalar=inv_rms[:, h : h + 1],
+                        in1=table[:, t, :, :],
+                        op0=ALU.mult,
+                        op1=ALU.mult,
+                    )
+                nc.gpsimd.tensor_tensor(
+                    out=stage[:, :, t, 0:HALF],
+                    in0=terms[:, :, 0, 0:HALF],
+                    in1=terms[:, :, 1, HALF:D],
+                    op=ALU.add,
+                )
+                nc.gpsimd.tensor_tensor(
+                    out=stage[:, :, t, HALF:D],
+                    in0=terms[:, :, 0, HALF:D],
+                    in1=terms[:, :, 1, 0:HALF],
+                    op=ALU.add,
+                )
+            if t == ROW_TILES - 1:
+                if w_block < 4:
+                    dst = out_views[0][:, w_block * ROW_TILES : (w_block + 1) * ROW_TILES, :]
+                else:
+                    dst = out_views[w_block - 3]
+                nc.sync.dma_start(out=dst, in_=stage[:].rearrange("p h t d -> p h (t d)"))
+
+        for s in range(MX_STEPS + LAG + 1):
+            banks = transpose_step(s) if s < PREP_STEPS else None
+            if 0 <= s - LAG < MX_STEPS:
+                matmul_step(s - LAG)
+            for i in range(2):
+                if 0 <= s - LAG - 1 < MX_STEPS:
+                    w_block, tile_pair = divmod(s - LAG - 1, 2)
+                    norm_and_rope(w_block, 2 * tile_pair + i)
+                if banks is not None:
+                    regroup_and_quantise(s, i, banks[2 * i : 2 * i + 2])

@@ -42,21 +42,21 @@ def tile_refattention_pa_kernel(
         words_pool = ctx.enter_context(tc.tile_pool(name="words", bufs=3))
         small = ctx.enter_context(tc.tile_pool(name="small", bufs=4))
         work = ctx.enter_context(tc.tile_pool(name="work", bufs=3))
-        stage_pool = ctx.enter_context(tc.tile_pool(name="stage", bufs=2))
+        stage_pool = ctx.enter_context(tc.tile_pool(name="stage", bufs=3))
         flip_psum = ctx.enter_context(tc.psum_pool(name="flip", bufs=4))
         acc_psum = ctx.enter_context(tc.psum_pool(name="acc", bufs=4))
         ctx.enter_context(tc.manual_schedule())
 
         gains_row = const.tile([P, 2 * D], BF16, name="gains_row")
         nc.vector.memset(gains_row[:], 0.0)
-        nc.scalar.dma_start(out=gains_row[0:1, 0:D], in_=q_norm_w.rearrange("(o d) -> o d", o=1))
-        nc.scalar.dma_start(out=gains_row[0:1, D : 2 * D], in_=k_norm_w.rearrange("(o d) -> o d", o=1))
+        nc.sync.dma_start(out=gains_row[0:1, 0:D], in_=q_norm_w.rearrange("(o d) -> o d", o=1))
+        nc.sync.dma_start(out=gains_row[0:1, D : 2 * D], in_=k_norm_w.rearrange("(o d) -> o d", o=1))
         cos_sb = const.tile([P, ROW_TILES, D], BF16, name="cos_sb")
         sin_sb = const.tile([P, ROW_TILES, D], BF16, name="sin_sb")
-        nc.scalar.dma_start(
+        nc.sync.dma_start(
             out=cos_sb[:], in_=cos.flatten_outer_dims().rearrange("(p t) d -> p t d", t=ROW_TILES)
         )
-        nc.scalar.dma_start(
+        nc.sync.dma_start(
             out=sin_sb[:], in_=sin.flatten_outer_dims().rearrange("(p t) d -> p t d", t=ROW_TILES)
         )
 
@@ -84,7 +84,7 @@ def tile_refattention_pa_kernel(
         eps_col = const.tile([P, 1], F32, name="eps_col")
         nc.vector.memset(eps_col[:], EPS)
         table_warm = const.tile([P, 1], F32, name="table_warm")
-        nc.scalar.activation(out=table_warm[:], in_=eps_col[:], func=ACT.Sqrt)
+        nc.scalar.activation(out=table_warm[:], in_=eps_col[:], func=ACT.Abs_reciprocal_sqrt)
 
         gains_ps = flip_psum.tile([P, 2 * D], F32, tag="flip", name="gains_ps")
         nc.tensor.matmul(out=gains_ps[:], lhsT=ones[:], rhs=gains_row[:], start=True, stop=True)
@@ -129,6 +129,9 @@ def tile_refattention_pa_kernel(
         scales = {}
         accs = {}
         stages = {}
+        grouped = {}
+        sum_sq = {}
+        inv_rms = {}
 
         def transpose_step(s):
             words = raw[s][:].bitcast(F32)
@@ -147,27 +150,30 @@ def tile_refattention_pa_kernel(
                     banks.append(bank)
             return banks
 
-        def regroup_and_quantise(s, local_pass, banks):
+        def copy_out(s, local_pass, pair, bank):
             block, k_half = divmod(s, 2)
-            if k_half == 0 and local_pass == 0:
+            if k_half == 0 and local_pass == 0 and pair == 0:
                 pool = const if block == 0 else words_pool
                 codes[block] = pool.tile([P, PASSES, BLOCK_ROWS], U32, align_bytes=64, name="codes")
                 scales[block] = pool.tile([P, PASSES, BLOCK_ROWS], U8, align_bytes=64, name="scales")
-            grouped = grouped_pool.tile([P, 4 * BLOCK_ROWS], BF16, align_bytes=64, name="grouped")
-            grouped_words = grouped[:].bitcast(F32)
-            for pair in range(2):
-                engine_copy = nc.vector.tensor_copy if (s <= LAG and pair == 1) else nc.scalar.copy
-                engine_copy(
-                    out=grouped_words[:, pair * 4 * P : (pair + 1) * 4 * P].rearrange(
-                        "p (c u) -> p c u", u=2
-                    ),
-                    in_=banks[pair][:].rearrange("p u c -> p c u"),
+            if pair == 0:
+                grouped[local_pass] = grouped_pool.tile(
+                    [P, 4 * BLOCK_ROWS], BF16, align_bytes=64, name="grouped"
                 )
+            grouped_words = grouped[local_pass][:].bitcast(F32)
+            engine_copy = nc.vector.tensor_copy if (s <= LAG and pair == 1) else nc.scalar.copy
+            engine_copy(
+                out=grouped_words[:, pair * 4 * P : (pair + 1) * 4 * P].rearrange("p (c u) -> p c u", u=2),
+                in_=bank[:].rearrange("p u c -> p c u"),
+            )
+
+        def quantise(s, local_pass):
+            block, k_half = divmod(s, 2)
             g = k_half * STEP_PASSES + local_pass
             nc.vector.quantize_mx(
                 out=codes[block][:, g, :].bitcast(FP8X4),
                 scales=scales[block][:, g, :],
-                in_=grouped[:],
+                in_=grouped[local_pass][:],
             )
 
         def matmul_step(m):
@@ -187,29 +193,39 @@ def tile_refattention_pa_kernel(
                     )
                 accs[(w_block, t)] = acc
 
-        def norm_and_rope(w_block, t):
+        def sum_squares(w_block, t):
             acc = accs[(w_block, t)]
-            if t == 0:
-                stages[w_block] = stage_pool.tile([P, ROW_TILES, ROW_TILES, D], F32, name="stage")
-            stage = stages[w_block]
             squares = work.tile([P, BLOCK_ROWS], F32, name="squares")
-            sum_sq = small.tile([P, ROW_TILES], F32, name="sum_sq")
+            sum_sq[t] = small.tile([P, ROW_TILES], F32, name="sum_sq")
             for h in range(ROW_TILES):
                 nc.scalar.activation(
                     out=squares[:, h * D : (h + 1) * D],
                     in_=acc[:, h * D : (h + 1) * D],
                     func=ACT.Square,
-                    accum_out=sum_sq[:, h : h + 1],
+                    accum_out=sum_sq[t][:, h : h + 1],
                 )
-            rms = small.tile([P, ROW_TILES], F32, name="rms")
-            nc.scalar.activation(out=rms[:], in_=sum_sq[:], func=ACT.Sqrt, bias=eps_col[:], scale=1.0 / D)
-            inv_rms = small.tile([P, ROW_TILES], F32, name="inv_rms")
-            nc.vector.reciprocal(out=inv_rms[:], in_=rms[:])
+
+        def inverse_rms(t):
+            inv_rms[t] = small.tile([P, ROW_TILES], F32, name="inv_rms")
+            nc.scalar.activation(
+                out=inv_rms[t][:],
+                in_=sum_sq[t][:],
+                func=ACT.Abs_reciprocal_sqrt,
+                bias=eps_col[:],
+                scale=1.0 / D,
+            )
+
+        def scale_and_rotate(w_block, t):
+            acc = accs[(w_block, t)]
+            tile_pair, i = divmod(t, 2)
+            if i == 0:
+                stages[w_block] = stage_pool.tile([P, ROW_TILES, 2, D], F32, name="stage")
+            stage = stages[w_block]
             if w_block == W_BLOCKS - 1:
                 nc.vector.tensor_tensor(
-                    out=stage[:, :, t, :],
+                    out=stage[:, :, i, :],
                     in0=acc[:].rearrange("p (h d) -> p h d", d=D),
-                    in1=inv_rms[:].unsqueeze(2).to_broadcast([P, ROW_TILES, D]),
+                    in1=inv_rms[t][:].unsqueeze(2).to_broadcast([P, ROW_TILES, D]),
                     op=ALU.mult,
                 )
             else:
@@ -219,37 +235,52 @@ def tile_refattention_pa_kernel(
                     nc.vector.scalar_tensor_tensor(
                         out=terms[:, h, :, :],
                         in0=acc[:, h * D : (h + 1) * D].unsqueeze(1).to_broadcast([P, 2, D]),
-                        scalar=inv_rms[:, h : h + 1],
+                        scalar=inv_rms[t][:, h : h + 1],
                         in1=table[:, t, :, :],
                         op0=ALU.mult,
                         op1=ALU.mult,
                     )
                 nc.gpsimd.tensor_tensor(
-                    out=stage[:, :, t, 0:HALF],
+                    out=stage[:, :, i, 0:HALF],
                     in0=terms[:, :, 0, 0:HALF],
                     in1=terms[:, :, 1, HALF:D],
                     op=ALU.add,
                 )
                 nc.gpsimd.tensor_tensor(
-                    out=stage[:, :, t, HALF:D],
+                    out=stage[:, :, i, HALF:D],
                     in0=terms[:, :, 0, HALF:D],
                     in1=terms[:, :, 1, 0:HALF],
                     op=ALU.add,
                 )
-            if t == ROW_TILES - 1:
+            if i == 1:
                 if w_block < 4:
-                    dst = out_views[0][:, w_block * ROW_TILES : (w_block + 1) * ROW_TILES, :]
+                    heads = out_views[0][:, w_block * ROW_TILES : (w_block + 1) * ROW_TILES, :]
                 else:
-                    dst = out_views[w_block - 3]
-                nc.sync.dma_start(out=dst, in_=stage[:].rearrange("p h t d -> p h (t d)"))
+                    heads = out_views[w_block - 3]
+                nc.sync.dma_start(
+                    out=heads[:, :, tile_pair * 2 * D : (tile_pair + 1) * 2 * D],
+                    in_=stage[:].rearrange("p h i d -> p h (i d)"),
+                )
 
         for s in range(MX_STEPS + LAG + 1):
-            banks = transpose_step(s) if s < PREP_STEPS else None
+            prepare = s < PREP_STEPS
+            finish = 0 <= s - LAG - 1 < MX_STEPS
+            w_block, tile_pair = divmod(s - LAG - 1, 2)
+            if prepare:
+                banks = transpose_step(s)
             if 0 <= s - LAG < MX_STEPS:
                 matmul_step(s - LAG)
             for i in range(2):
-                if 0 <= s - LAG - 1 < MX_STEPS:
-                    w_block, tile_pair = divmod(s - LAG - 1, 2)
-                    norm_and_rope(w_block, 2 * tile_pair + i)
-                if banks is not None:
-                    regroup_and_quantise(s, i, banks[2 * i : 2 * i + 2])
+                t = 2 * tile_pair + i
+                if finish:
+                    sum_squares(w_block, t)
+                if prepare:
+                    copy_out(s, i, 0, banks[2 * i])
+                if finish:
+                    inverse_rms(t)
+                if prepare:
+                    copy_out(s, i, 1, banks[2 * i + 1])
+                if finish:
+                    scale_and_rotate(w_block, t)
+                if prepare:
+                    quantise(s, i)

@@ -13,22 +13,23 @@ ALU = mybir.AluOpType
 
 P = 128
 TOKENS = 512
+TOKEN_TILES = TOKENS // P
 HID = 2048
 D = 128
 HALF = D // 2
 EPS = 1e-6
-BLOCK_ROWS = 512
-ROW_TILES = BLOCK_ROWS // P
 PASSES = HID // 512
-STEP_K = HID // 2
-STEP_PASSES = STEP_K // 512
 PASS_WORDS = 256
-W_BLOCKS = 6
-PREP_STEPS = 2 * (W_BLOCKS + 1)
-MX_STEPS = 2 * W_BLOCKS
-LAG = 4
+UNIT_ROWS = 256
+UNIT_TILES = UNIT_ROWS // P
+X_UNITS = TOKENS // UNIT_ROWS
+Q_UNITS, K_UNITS, V_UNITS = 8, 2, 2
+W_UNITS = Q_UNITS + K_UNITS + V_UNITS
+UNITS = X_UNITS + W_UNITS
+LAG = 3
+LOADS_AHEAD = 6
 
-FLOPS = 2 * TOKENS * HID * (W_BLOCKS * BLOCK_ROWS)
+FLOPS = 2 * TOKENS * HID * (W_UNITS * UNIT_ROWS)
 
 
 def tile_refattention_pa_kernel(
@@ -39,9 +40,10 @@ def tile_refattention_pa_kernel(
         const = ctx.enter_context(tc.tile_pool(name="const", bufs=1))
         raw_pool = ctx.enter_context(tc.tile_pool(name="raw", bufs=1))
         grouped_pool = ctx.enter_context(tc.tile_pool(name="grouped", bufs=4))
-        words_pool = ctx.enter_context(tc.tile_pool(name="words", bufs=3))
-        small = ctx.enter_context(tc.tile_pool(name="small", bufs=4))
-        work = ctx.enter_context(tc.tile_pool(name="work", bufs=3))
+        words_pool = ctx.enter_context(tc.tile_pool(name="words", bufs=4))
+        small = ctx.enter_context(tc.tile_pool(name="small", bufs=3))
+        squares_pool = ctx.enter_context(tc.tile_pool(name="squares", bufs=3))
+        terms_pool = ctx.enter_context(tc.tile_pool(name="terms", bufs=2))
         stage_pool = ctx.enter_context(tc.tile_pool(name="stage", bufs=3))
         flip_psum = ctx.enter_context(tc.psum_pool(name="flip", bufs=4))
         acc_psum = ctx.enter_context(tc.psum_pool(name="acc", bufs=4))
@@ -51,31 +53,30 @@ def tile_refattention_pa_kernel(
         nc.vector.memset(gains_row[:], 0.0)
         nc.sync.dma_start(out=gains_row[0:1, 0:D], in_=q_norm_w.rearrange("(o d) -> o d", o=1))
         nc.sync.dma_start(out=gains_row[0:1, D : 2 * D], in_=k_norm_w.rearrange("(o d) -> o d", o=1))
-        cos_sb = const.tile([P, ROW_TILES, D], BF16, name="cos_sb")
-        sin_sb = const.tile([P, ROW_TILES, D], BF16, name="sin_sb")
+        cos_sb = const.tile([P, TOKEN_TILES, D], BF16, name="cos_sb")
+        sin_sb = const.tile([P, TOKEN_TILES, D], BF16, name="sin_sb")
         nc.sync.dma_start(
-            out=cos_sb[:], in_=cos.flatten_outer_dims().rearrange("(p t) d -> p t d", t=ROW_TILES)
+            out=cos_sb[:], in_=cos.flatten_outer_dims().rearrange("(p t) d -> p t d", t=TOKEN_TILES)
         )
         nc.sync.dma_start(
-            out=sin_sb[:], in_=sin.flatten_outer_dims().rearrange("(p t) d -> p t d", t=ROW_TILES)
+            out=sin_sb[:], in_=sin.flatten_outer_dims().rearrange("(p t) d -> p t d", t=TOKEN_TILES)
         )
 
-        x_rows = hidden_states.flatten_outer_dims().rearrange("(p t) k -> p t k", t=ROW_TILES)
-        row_views = [x_rows]
-        for j in range(4):
-            rows = Wq[j * BLOCK_ROWS : (j + 1) * BLOCK_ROWS, :]
-            row_views.append(rows.rearrange("(r p) k -> p r k", p=P))
-        row_views.append(Wk.rearrange("(r p) k -> p r k", p=P))
-        row_views.append(Wv.rearrange("(r p) k -> p r k", p=P))
-        raw = []
-        for s in range(PREP_STEPS):
-            block, k_half = divmod(s, 2)
-            raw_tile = raw_pool.tile([P, ROW_TILES, STEP_K], BF16, name="raw%d" % s)
-            nc.sync.dma_start(
-                out=raw_tile[:],
-                in_=row_views[block][:, :, k_half * STEP_K : (k_half + 1) * STEP_K],
-            )
-            raw.append(raw_tile)
+        x_rows = hidden_states.flatten_outer_dims().rearrange("(p t) k -> p t k", t=TOKEN_TILES)
+        unit_rows = [x_rows[:, i * UNIT_TILES : (i + 1) * UNIT_TILES, :] for i in range(X_UNITS)]
+        for weight, units in ((Wq, Q_UNITS), (Wk, K_UNITS), (Wv, V_UNITS)):
+            for i in range(units):
+                rows = weight[i * UNIT_ROWS : (i + 1) * UNIT_ROWS, :]
+                unit_rows.append(rows.rearrange("(r p) k -> p r k", p=P))
+
+        raw = {}
+
+        def load(unit):
+            raw[unit] = raw_pool.tile([P, UNIT_TILES, HID], BF16, name="raw%d" % unit)
+            nc.sync.dma_start(out=raw[unit][:], in_=unit_rows[unit])
+
+        for unit in range(LOADS_AHEAD):
+            load(unit)
 
         ident = const.tile([P, P], F32, name="ident")
         make_identity(nc, ident[:])
@@ -96,17 +97,17 @@ def tile_refattention_pa_kernel(
         rope = []
         for which in range(2):
             first = which * D
-            table = const.tile([P, ROW_TILES, 2, D], F32, name="rope%d" % which)
+            table = const.tile([P, TOKEN_TILES, 2, D], F32, name="rope%d" % which)
             nc.gpsimd.tensor_tensor(
                 out=table[:, :, 0, :],
                 in0=cos_sb[:],
-                in1=gains[:, first : first + D].unsqueeze(1).to_broadcast([P, ROW_TILES, D]),
+                in1=gains[:, first : first + D].unsqueeze(1).to_broadcast([P, TOKEN_TILES, D]),
                 op=ALU.mult,
             )
             nc.gpsimd.tensor_tensor(
                 out=table[:, :, 1, 0:HALF],
                 in0=sin_sb[:, :, HALF:D],
-                in1=gains[:, first : first + HALF].unsqueeze(1).to_broadcast([P, ROW_TILES, HALF]),
+                in1=gains[:, first : first + HALF].unsqueeze(1).to_broadcast([P, TOKEN_TILES, HALF]),
                 op=ALU.mult,
             )
             nc.gpsimd.tensor_tensor(
@@ -114,173 +115,188 @@ def tile_refattention_pa_kernel(
                 in0=sin_sb[:, :, 0:HALF],
                 in1=minus_gains[:, first + HALF : first + D]
                 .unsqueeze(1)
-                .to_broadcast([P, ROW_TILES, HALF]),
+                .to_broadcast([P, TOKEN_TILES, HALF]),
                 op=ALU.mult,
             )
             rope.append(table)
 
-        out_views = [
-            out_0.rearrange("o h (p t) d -> p (o h) (t d)", t=ROW_TILES),
-            out_1.rearrange("o h (p t) d -> p (o h) (t d)", t=ROW_TILES),
-            out_2.rearrange("o h (p t) d -> p (o h) (t d)", t=ROW_TILES),
-        ]
+        unit_out = []
+        for out, units in ((out_0, Q_UNITS), (out_1, K_UNITS), (out_2, V_UNITS)):
+            heads = out.rearrange("o h (p t) d -> p (o h) (t d)", t=TOKEN_TILES)
+            for i in range(units):
+                unit_out.append(heads[:, i * UNIT_TILES : (i + 1) * UNIT_TILES, :])
 
+        banks = {}
+        grouped = {}
         codes = {}
         scales = {}
         accs = {}
-        stages = {}
-        grouped = {}
         sum_sq = {}
         inv_rms = {}
+        terms = {}
+        stages = {}
 
-        def transpose_step(s):
-            words = raw[s][:].bitcast(F32)
-            banks = []
-            for local_pass in range(STEP_PASSES):
-                for pair in range(2):
-                    bank = flip_psum.tile([P, 2, 2 * P], F32, tag="flip", name="bank")
-                    for r in range(2):
-                        for u in range(2):
-                            first = local_pass * PASS_WORDS + u * P
-                            nc.tensor.transpose(
-                                bank[:, u, r * P : (r + 1) * P],
-                                words[:, 2 * pair + r, first : first + P],
-                                ident[:],
-                            )
-                    banks.append(bank)
-            return banks
+        def transposes(unit):
+            words = raw[unit][:].bitcast(F32)
+            for g in range(PASSES):
+                bank = flip_psum.tile([P, 2, UNIT_ROWS], F32, tag="flip", name="bank")
+                for r in range(UNIT_TILES):
+                    for u in range(2):
+                        first = g * PASS_WORDS + u * P
+                        nc.tensor.transpose(
+                            bank[:, u, r * P : (r + 1) * P], words[:, r, first : first + P], ident[:]
+                        )
+                banks[(unit, g)] = bank
 
-        def copy_out(s, local_pass, pair, bank):
-            block, k_half = divmod(s, 2)
-            if k_half == 0 and local_pass == 0 and pair == 0:
-                pool = const if block == 0 else words_pool
-                codes[block] = pool.tile([P, PASSES, BLOCK_ROWS], U32, align_bytes=64, name="codes")
-                scales[block] = pool.tile([P, PASSES, BLOCK_ROWS], U8, align_bytes=64, name="scales")
-            if pair == 0:
-                grouped[local_pass] = grouped_pool.tile(
-                    [P, 4 * BLOCK_ROWS], BF16, align_bytes=64, name="grouped"
+        def copy_out(unit, g):
+            pair, i = divmod(g, 2)
+            if i == 0:
+                grouped[(unit, pair)] = grouped_pool.tile(
+                    [P, 2 * 4 * UNIT_ROWS], BF16, align_bytes=64, name="grouped"
                 )
-            grouped_words = grouped[local_pass][:].bitcast(F32)
-            engine_copy = nc.vector.tensor_copy if (s <= LAG and pair == 1) else nc.scalar.copy
+            grouped_words = grouped[(unit, pair)][:].bitcast(F32)
+            engine_copy = nc.vector.tensor_copy if (unit <= LAG and i == 1) else nc.scalar.copy
             engine_copy(
-                out=grouped_words[:, pair * 4 * P : (pair + 1) * 4 * P].rearrange("p (c u) -> p c u", u=2),
-                in_=bank[:].rearrange("p u c -> p c u"),
+                out=grouped_words[:, i * 2 * UNIT_ROWS : (i + 1) * 2 * UNIT_ROWS].rearrange(
+                    "p (c u) -> p c u", u=2
+                ),
+                in_=banks[(unit, g)][:].rearrange("p u c -> p c u"),
             )
 
-        def quantise(s, local_pass):
-            block, k_half = divmod(s, 2)
-            g = k_half * STEP_PASSES + local_pass
-            nc.vector.quantize_mx(
-                out=codes[block][:, g, :].bitcast(FP8X4),
-                scales=scales[block][:, g, :],
-                in_=grouped[local_pass][:],
-            )
-
-        def matmul_step(m):
-            w_block, tile_pair = divmod(m, 2)
-            for i in range(2):
-                t = 2 * tile_pair + i
-                acc = acc_psum.tile([P, BLOCK_ROWS], F32, tag="acc", name="acc")
-                for g in range(PASSES):
-                    nc.tensor.matmul_mx(
-                        out=acc[:],
-                        lhsT=codes[0][:, g, t * P : (t + 1) * P].bitcast(FP8X4),
-                        lhsT_scale=scales[0][:, g, t * P : (t + 1) * P],
-                        rhs=codes[w_block + 1][:, g, :].bitcast(FP8X4),
-                        rhs_scale=scales[w_block + 1][:, g, :],
-                        start=(g == 0),
-                        stop=(g == PASSES - 1),
-                    )
-                accs[(w_block, t)] = acc
-
-        def sum_squares(w_block, t):
-            acc = accs[(w_block, t)]
-            squares = work.tile([P, BLOCK_ROWS], F32, name="squares")
-            sum_sq[t] = small.tile([P, ROW_TILES], F32, name="sum_sq")
-            for h in range(ROW_TILES):
-                nc.scalar.activation(
-                    out=squares[:, h * D : (h + 1) * D],
-                    in_=acc[:, h * D : (h + 1) * D],
-                    func=ACT.Square,
-                    accum_out=sum_sq[t][:, h : h + 1],
+        def quantise(unit, pair):
+            if pair == 0:
+                pool = const if unit < X_UNITS else words_pool
+                codes[unit] = pool.tile(
+                    [P, PASSES * UNIT_ROWS], U32, align_bytes=64, name="codes%d" % min(unit, X_UNITS)
                 )
+                scales[unit] = pool.tile(
+                    [P, PASSES * UNIT_ROWS], U8, align_bytes=64, name="scales%d" % min(unit, X_UNITS)
+                )
+            columns = slice(pair * 2 * UNIT_ROWS, (pair + 1) * 2 * UNIT_ROWS)
+            nc.vector.quantize_mx(
+                out=codes[unit][:, columns].bitcast(FP8X4),
+                scales=scales[unit][:, columns],
+                in_=grouped[(unit, pair)][:],
+            )
 
-        def inverse_rms(t):
-            inv_rms[t] = small.tile([P, ROW_TILES], F32, name="inv_rms")
+        def matmuls(m):
+            w = m + X_UNITS
+            for x_unit in range(X_UNITS):
+                acc = acc_psum.tile([P, UNIT_TILES, UNIT_ROWS], F32, tag="acc", name="acc")
+                for i in range(UNIT_TILES):
+                    for g in range(PASSES):
+                        tokens = slice(g * UNIT_ROWS + i * P, g * UNIT_ROWS + (i + 1) * P)
+                        features = slice(g * UNIT_ROWS, (g + 1) * UNIT_ROWS)
+                        nc.tensor.matmul_mx(
+                            out=acc[:, i, :],
+                            lhsT=codes[x_unit][:, tokens].bitcast(FP8X4),
+                            lhsT_scale=scales[x_unit][:, tokens],
+                            rhs=codes[w][:, features].bitcast(FP8X4),
+                            rhs_scale=scales[w][:, features],
+                            start=(g == 0),
+                            stop=(g == PASSES - 1),
+                        )
+                accs[(m, x_unit)] = acc
+
+        def sum_squares(m, x_unit):
+            acc = accs[(m, x_unit)]
+            if x_unit == 0:
+                sum_sq[m] = small.tile([P, UNIT_TILES * TOKEN_TILES], F32, name="sum_sq")
+            squares = squares_pool.tile([P, UNIT_TILES, UNIT_ROWS], F32, name="squares")
+            for i in range(UNIT_TILES):
+                for h in range(UNIT_TILES):
+                    column = h * TOKEN_TILES + x_unit * UNIT_TILES + i
+                    nc.scalar.activation(
+                        out=squares[:, i, h * D : (h + 1) * D],
+                        in_=acc[:, i, h * D : (h + 1) * D],
+                        func=ACT.Square,
+                        accum_out=sum_sq[m][:, column : column + 1],
+                    )
+
+        def inverse_rms(m):
+            inv_rms[m] = small.tile([P, UNIT_TILES * TOKEN_TILES], F32, name="inv_rms")
             nc.scalar.activation(
-                out=inv_rms[t][:],
-                in_=sum_sq[t][:],
+                out=inv_rms[m][:],
+                in_=sum_sq[m][:],
                 func=ACT.Abs_reciprocal_sqrt,
                 bias=eps_col[:],
                 scale=1.0 / D,
             )
 
-        def scale_and_rotate(w_block, t):
-            acc = accs[(w_block, t)]
-            tile_pair, i = divmod(t, 2)
-            if i == 0:
-                stages[w_block] = stage_pool.tile([P, ROW_TILES, 2, D], F32, name="stage")
-            stage = stages[w_block]
-            if w_block == W_BLOCKS - 1:
+        def scale_bank(m, x_unit):
+            acc = accs[(m, x_unit)]
+            if x_unit == 0:
+                stages[m] = stage_pool.tile([P, UNIT_TILES, TOKEN_TILES, D], F32, name="stage")
+            if m >= Q_UNITS + K_UNITS:
+                tiles = slice(x_unit * UNIT_TILES, (x_unit + 1) * UNIT_TILES)
                 nc.vector.tensor_tensor(
-                    out=stage[:, :, i, :],
-                    in0=acc[:].rearrange("p (h d) -> p h d", d=D),
-                    in1=inv_rms[t][:].unsqueeze(2).to_broadcast([P, ROW_TILES, D]),
+                    out=stages[m][:, :, tiles, :],
+                    in0=acc[:].rearrange("p i (h d) -> p h i d", d=D),
+                    in1=inv_rms[m][:]
+                    .rearrange("p (h t) -> p h t", t=TOKEN_TILES)[:, :, tiles]
+                    .unsqueeze(3)
+                    .to_broadcast([P, UNIT_TILES, UNIT_TILES, D]),
                     op=ALU.mult,
                 )
-            else:
-                table = rope[0] if w_block < 4 else rope[1]
-                terms = work.tile([P, ROW_TILES, 2, D], F32, name="terms")
-                for h in range(ROW_TILES):
+                return
+            if x_unit == 0:
+                terms[m] = terms_pool.tile([P, UNIT_TILES, TOKEN_TILES, 2, D], F32, name="terms")
+            table = rope[0] if m < Q_UNITS else rope[1]
+            for i in range(UNIT_TILES):
+                t = x_unit * UNIT_TILES + i
+                for h in range(UNIT_TILES):
+                    column = h * TOKEN_TILES + t
                     nc.vector.scalar_tensor_tensor(
-                        out=terms[:, h, :, :],
-                        in0=acc[:, h * D : (h + 1) * D].unsqueeze(1).to_broadcast([P, 2, D]),
-                        scalar=inv_rms[t][:, h : h + 1],
+                        out=terms[m][:, h, t, :, :],
+                        in0=acc[:, i, h * D : (h + 1) * D].unsqueeze(1).to_broadcast([P, 2, D]),
+                        scalar=inv_rms[m][:, column : column + 1],
                         in1=table[:, t, :, :],
                         op0=ALU.mult,
                         op1=ALU.mult,
                     )
-                nc.gpsimd.tensor_tensor(
-                    out=stage[:, :, i, 0:HALF],
-                    in0=terms[:, :, 0, 0:HALF],
-                    in1=terms[:, :, 1, HALF:D],
-                    op=ALU.add,
-                )
-                nc.gpsimd.tensor_tensor(
-                    out=stage[:, :, i, HALF:D],
-                    in0=terms[:, :, 0, HALF:D],
-                    in1=terms[:, :, 1, 0:HALF],
-                    op=ALU.add,
-                )
-            if i == 1:
-                if w_block < 4:
-                    heads = out_views[0][:, w_block * ROW_TILES : (w_block + 1) * ROW_TILES, :]
-                else:
-                    heads = out_views[w_block - 3]
-                nc.sync.dma_start(
-                    out=heads[:, :, tile_pair * 2 * D : (tile_pair + 1) * 2 * D],
-                    in_=stage[:].rearrange("p h i d -> p h (i d)"),
-                )
 
-        for s in range(MX_STEPS + LAG + 1):
-            prepare = s < PREP_STEPS
-            finish = 0 <= s - LAG - 1 < MX_STEPS
-            w_block, tile_pair = divmod(s - LAG - 1, 2)
+        def add_and_store(m):
+            if m < Q_UNITS + K_UNITS:
+                nc.gpsimd.tensor_tensor(
+                    out=stages[m][:, :, :, 0:HALF],
+                    in0=terms[m][:, :, :, 0, 0:HALF],
+                    in1=terms[m][:, :, :, 1, HALF:D],
+                    op=ALU.add,
+                )
+                nc.gpsimd.tensor_tensor(
+                    out=stages[m][:, :, :, HALF:D],
+                    in0=terms[m][:, :, :, 0, HALF:D],
+                    in1=terms[m][:, :, :, 1, 0:HALF],
+                    op=ALU.add,
+                )
+            nc.sync.dma_start(out=unit_out[m], in_=stages[m][:].rearrange("p h t d -> p h (t d)"))
+
+        for s in range(W_UNITS + LAG + 1):
+            m = s - LAG
+            prepare = s < UNITS
+            multiply = 0 <= m < W_UNITS
+            finish = 0 <= m - 1 < W_UNITS
+            if s + LOADS_AHEAD < UNITS:
+                load(s + LOADS_AHEAD)
             if prepare:
-                banks = transpose_step(s)
-            if 0 <= s - LAG < MX_STEPS:
-                matmul_step(s - LAG)
-            for i in range(2):
-                t = 2 * tile_pair + i
-                if finish:
-                    sum_squares(w_block, t)
-                if prepare:
-                    copy_out(s, i, 0, banks[2 * i])
-                if finish:
-                    inverse_rms(t)
-                if prepare:
-                    copy_out(s, i, 1, banks[2 * i + 1])
-                if finish:
-                    scale_and_rotate(w_block, t)
-                if prepare:
-                    quantise(s, i)
+                transposes(s)
+            if multiply:
+                matmuls(m)
+            if finish:
+                sum_squares(m - 1, 1)
+            if prepare:
+                copy_out(s, 0)
+            if finish:
+                inverse_rms(m - 1)
+            if prepare:
+                for g in range(1, PASSES):
+                    copy_out(s, g)
+            if multiply:
+                sum_squares(m, 0)
+            if finish:
+                scale_bank(m - 1, 0)
+                scale_bank(m - 1, 1)
+                add_and_store(m - 1)
+            if prepare:
+                quantise(s, 0)
+                quantise(s, 1)

@@ -29,6 +29,9 @@ UNITS = X_UNITS + W_UNITS
 LAG = 3
 LOADS_AHEAD = 6
 
+WARM_FIRST = 6
+WARM_PER_UNIT = 2
+
 FLOPS = 2 * TOKENS * HID * (W_UNITS * UNIT_ROWS)
 
 
@@ -86,6 +89,16 @@ def tile_refattention_pa_kernel(
         nc.vector.memset(eps_col[:], EPS)
         table_warm = const.tile([P, 1], F32, name="table_warm")
         nc.scalar.activation(out=table_warm[:], in_=eps_col[:], func=ACT.Abs_reciprocal_sqrt)
+
+        warm_rhs = const.tile([P, 4 * P], BF16, name="warm_rhs")
+        nc.vector.memset(warm_rhs[:], 0.0)
+        warm_ps = acc_psum.tile([P, 4 * P], F32, tag="acc", name="warm_ps")
+
+        def keep_clock_up(count):
+            for i in range(count):
+                nc.tensor.matmul(out=warm_ps[:], lhsT=ones[:], rhs=warm_rhs[:], start=True, stop=True)
+
+        keep_clock_up(WARM_FIRST)
 
         gains_ps = flip_psum.tile([P, 2 * D], F32, tag="flip", name="gains_ps")
         nc.tensor.matmul(out=gains_ps[:], lhsT=ones[:], rhs=gains_row[:], start=True, stop=True)
@@ -282,6 +295,8 @@ def tile_refattention_pa_kernel(
                 transposes(s)
             if multiply:
                 matmuls(m)
+            elif prepare:
+                keep_clock_up(WARM_PER_UNIT)
             if finish:
                 sum_squares(m - 1, 1)
             if prepare:

@@ -29,9 +29,6 @@ UNITS = X_UNITS + W_UNITS
 LAG = 3
 LOADS_AHEAD = 6
 
-WARM_FIRST = 6
-WARM_PER_UNIT = 2
-
 FLOPS = 2 * TOKENS * HID * (W_UNITS * UNIT_ROWS)
 
 
@@ -44,7 +41,7 @@ def tile_refattention_pa_kernel(
         raw_pool = ctx.enter_context(tc.tile_pool(name="raw", bufs=1))
         grouped_pool = ctx.enter_context(tc.tile_pool(name="grouped", bufs=4))
         words_pool = ctx.enter_context(tc.tile_pool(name="words", bufs=4))
-        small = ctx.enter_context(tc.tile_pool(name="small", bufs=3))
+        small = ctx.enter_context(tc.tile_pool(name="small", bufs=6))
         squares_pool = ctx.enter_context(tc.tile_pool(name="squares", bufs=3))
         terms_pool = ctx.enter_context(tc.tile_pool(name="terms", bufs=2))
         stage_pool = ctx.enter_context(tc.tile_pool(name="stage", bufs=3))
@@ -90,16 +87,6 @@ def tile_refattention_pa_kernel(
         table_warm = const.tile([P, 1], F32, name="table_warm")
         nc.scalar.activation(out=table_warm[:], in_=eps_col[:], func=ACT.Abs_reciprocal_sqrt)
 
-        warm_rhs = const.tile([P, 4 * P], BF16, name="warm_rhs")
-        nc.vector.memset(warm_rhs[:], 0.0)
-        warm_ps = acc_psum.tile([P, 4 * P], F32, tag="acc", name="warm_ps")
-
-        def keep_clock_up(count):
-            for i in range(count):
-                nc.tensor.matmul(out=warm_ps[:], lhsT=ones[:], rhs=warm_rhs[:], start=True, stop=True)
-
-        keep_clock_up(WARM_FIRST)
-
         gains_ps = flip_psum.tile([P, 2 * D], F32, tag="flip", name="gains_ps")
         nc.tensor.matmul(out=gains_ps[:], lhsT=ones[:], rhs=gains_row[:], start=True, stop=True)
         gains = const.tile([P, 2 * D], F32, name="gains")
@@ -109,28 +96,21 @@ def tile_refattention_pa_kernel(
 
         rope = []
         for which in range(2):
-            first = which * D
+            w_lo = slice(which * D, which * D + HALF)
+            w_hi = slice(which * D + HALF, (which + 1) * D)
             table = const.tile([P, TOKEN_TILES, 2, D], F32, name="rope%d" % which)
-            nc.gpsimd.tensor_tensor(
-                out=table[:, :, 0, :],
-                in0=cos_sb[:],
-                in1=gains[:, first : first + D].unsqueeze(1).to_broadcast([P, TOKEN_TILES, D]),
-                op=ALU.mult,
-            )
-            nc.gpsimd.tensor_tensor(
-                out=table[:, :, 1, 0:HALF],
-                in0=sin_sb[:, :, HALF:D],
-                in1=gains[:, first : first + HALF].unsqueeze(1).to_broadcast([P, TOKEN_TILES, HALF]),
-                op=ALU.mult,
-            )
-            nc.gpsimd.tensor_tensor(
-                out=table[:, :, 1, HALF:D],
-                in0=sin_sb[:, :, 0:HALF],
-                in1=minus_gains[:, first + HALF : first + D]
-                .unsqueeze(1)
-                .to_broadcast([P, TOKEN_TILES, HALF]),
-                op=ALU.mult,
-            )
+            for row, columns, angles, gain in (
+                (0, slice(0, HALF), cos_sb[:, :, 0:HALF], gains[:, w_lo]),
+                (0, slice(HALF, D), sin_sb[:, :, 0:HALF], minus_gains[:, w_hi]),
+                (1, slice(0, HALF), sin_sb[:, :, HALF:D], gains[:, w_lo]),
+                (1, slice(HALF, D), cos_sb[:, :, HALF:D], gains[:, w_hi]),
+            ):
+                nc.gpsimd.tensor_tensor(
+                    out=table[:, :, row, columns],
+                    in0=angles,
+                    in1=gain.unsqueeze(1).to_broadcast([P, TOKEN_TILES, HALF]),
+                    op=ALU.mult,
+                )
             rope.append(table)
 
         unit_out = []
@@ -213,24 +193,23 @@ def tile_refattention_pa_kernel(
 
         def sum_squares(m, x_unit):
             acc = accs[(m, x_unit)]
-            if x_unit == 0:
-                sum_sq[m] = small.tile([P, UNIT_TILES * TOKEN_TILES], F32, name="sum_sq")
+            sum_sq[(m, x_unit)] = small.tile([P, UNIT_TILES * UNIT_TILES], F32, name="sum_sq")
             squares = squares_pool.tile([P, UNIT_TILES, UNIT_ROWS], F32, name="squares")
             for i in range(UNIT_TILES):
                 for h in range(UNIT_TILES):
-                    column = h * TOKEN_TILES + x_unit * UNIT_TILES + i
+                    column = i * UNIT_TILES + h
                     nc.scalar.activation(
                         out=squares[:, i, h * D : (h + 1) * D],
                         in_=acc[:, i, h * D : (h + 1) * D],
                         func=ACT.Square,
-                        accum_out=sum_sq[m][:, column : column + 1],
+                        accum_out=sum_sq[(m, x_unit)][:, column : column + 1],
                     )
 
-        def inverse_rms(m):
-            inv_rms[m] = small.tile([P, UNIT_TILES * TOKEN_TILES], F32, name="inv_rms")
+        def inverse_rms(m, x_unit):
+            inv_rms[(m, x_unit)] = small.tile([P, UNIT_TILES * UNIT_TILES], F32, name="inv_rms")
             nc.scalar.activation(
-                out=inv_rms[m][:],
-                in_=sum_sq[m][:],
+                out=inv_rms[(m, x_unit)][:],
+                in_=sum_sq[(m, x_unit)][:],
                 func=ACT.Abs_reciprocal_sqrt,
                 bias=eps_col[:],
                 scale=1.0 / D,
@@ -238,6 +217,7 @@ def tile_refattention_pa_kernel(
 
         def scale_bank(m, x_unit):
             acc = accs[(m, x_unit)]
+            inv = inv_rms[(m, x_unit)]
             if x_unit == 0:
                 stages[m] = stage_pool.tile([P, UNIT_TILES, TOKEN_TILES, D], F32, name="stage")
             if m >= Q_UNITS + K_UNITS:
@@ -245,11 +225,15 @@ def tile_refattention_pa_kernel(
                 nc.vector.tensor_tensor(
                     out=stages[m][:, :, tiles, :],
                     in0=acc[:].rearrange("p i (h d) -> p h i d", d=D),
-                    in1=inv_rms[m][:]
-                    .rearrange("p (h t) -> p h t", t=TOKEN_TILES)[:, :, tiles]
+                    in1=inv[:]
+                    .rearrange("p (i h) -> p h i", h=UNIT_TILES)
                     .unsqueeze(3)
                     .to_broadcast([P, UNIT_TILES, UNIT_TILES, D]),
                     op=ALU.mult,
+                )
+                nc.sync.dma_start(
+                    out=unit_out[m][:, :, x_unit * UNIT_ROWS : (x_unit + 1) * UNIT_ROWS],
+                    in_=stages[m][:, :, tiles, :].rearrange("p h i d -> p h (i d)"),
                 )
                 return
             if x_unit == 0:
@@ -258,30 +242,26 @@ def tile_refattention_pa_kernel(
             for i in range(UNIT_TILES):
                 t = x_unit * UNIT_TILES + i
                 for h in range(UNIT_TILES):
-                    column = h * TOKEN_TILES + t
+                    column = i * UNIT_TILES + h
                     nc.vector.scalar_tensor_tensor(
                         out=terms[m][:, h, t, :, :],
                         in0=acc[:, i, h * D : (h + 1) * D].unsqueeze(1).to_broadcast([P, 2, D]),
-                        scalar=inv_rms[m][:, column : column + 1],
+                        scalar=inv[:, column : column + 1],
                         in1=table[:, t, :, :],
                         op0=ALU.mult,
                         op1=ALU.mult,
                     )
 
-        def add_and_store(m):
-            if m < Q_UNITS + K_UNITS:
-                nc.gpsimd.tensor_tensor(
-                    out=stages[m][:, :, :, 0:HALF],
-                    in0=terms[m][:, :, :, 0, 0:HALF],
-                    in1=terms[m][:, :, :, 1, HALF:D],
-                    op=ALU.add,
-                )
-                nc.gpsimd.tensor_tensor(
-                    out=stages[m][:, :, :, HALF:D],
-                    in0=terms[m][:, :, :, 0, HALF:D],
-                    in1=terms[m][:, :, :, 1, 0:HALF],
-                    op=ALU.add,
-                )
+        def add_terms(m):
+            pairs = terms[m][:].rearrange("p h t r (c j) -> p (h t r) c j", j=HALF)
+            nc.gpsimd.tensor_tensor(
+                out=stages[m][:].rearrange("p h t (r j) -> p (h t r) j", j=HALF),
+                in0=pairs[:, :, 0, :],
+                in1=pairs[:, :, 1, :],
+                op=ALU.add,
+            )
+
+        def store(m):
             nc.sync.dma_start(out=unit_out[m], in_=stages[m][:].rearrange("p h t d -> p h (t d)"))
 
         for s in range(W_UNITS + LAG + 1):
@@ -295,14 +275,13 @@ def tile_refattention_pa_kernel(
                 transposes(s)
             if multiply:
                 matmuls(m)
-            elif prepare:
-                keep_clock_up(WARM_PER_UNIT)
             if finish:
                 sum_squares(m - 1, 1)
+                inverse_rms(m - 1, 0)
             if prepare:
                 copy_out(s, 0)
             if finish:
-                inverse_rms(m - 1)
+                inverse_rms(m - 1, 1)
             if prepare:
                 for g in range(1, PASSES):
                     copy_out(s, g)
@@ -311,7 +290,10 @@ def tile_refattention_pa_kernel(
             if finish:
                 scale_bank(m - 1, 0)
                 scale_bank(m - 1, 1)
-                add_and_store(m - 1)
+                if m - 1 < Q_UNITS + K_UNITS:
+                    add_terms(m - 1)
+            if 0 <= m - 2 < Q_UNITS + K_UNITS:
+                store(m - 2)
             if prepare:
                 quantise(s, 0)
                 quantise(s, 1)

from contextlib import ExitStack

import concourse.mybir as mybir
from concourse.masks import make_identity

F32 = mybir.dt.float32
BF16 = mybir.dt.bfloat16
U32 = mybir.dt.uint32
U8 = mybir.dt.uint8
FP8X4 = mybir.dt.float8_e4m3fn_x4
ACT = mybir.ActivationFunctionType
ALU = mybir.AluOpType

P = 128
TOKENS = 512
TOKEN_TILES = TOKENS // P
HID = 2048
D = 128
HALF = D // 2
EPS = 1e-6
PASSES = HID // 512
PASS_WORDS = 256
UNIT_ROWS = 256
UNIT_TILES = UNIT_ROWS // P
X_UNITS = TOKENS // UNIT_ROWS
Q_UNITS, K_UNITS, V_UNITS = 8, 2, 2
W_UNITS = Q_UNITS + K_UNITS + V_UNITS
UNITS = X_UNITS + W_UNITS
LAG = 3
LOADS_AHEAD = 6

FLOPS = 2 * TOKENS * HID * (W_UNITS * UNIT_ROWS)


def tile_refattention_pa_kernel(
    tc, hidden_states, cos, sin, Wq, Wk, Wv, q_norm_w, k_norm_w, out_0, out_1, out_2
):
    nc = tc.nc
    with ExitStack() as ctx:
        const = ctx.enter_context(tc.tile_pool(name="const", bufs=1))
        raw_pool = ctx.enter_context(tc.tile_pool(name="raw", bufs=1))
        grouped_pool = ctx.enter_context(tc.tile_pool(name="grouped", bufs=4))
        words_pool = ctx.enter_context(tc.tile_pool(name="words", bufs=4))
        small = ctx.enter_context(tc.tile_pool(name="small", bufs=6))
        squares_pool = ctx.enter_context(tc.tile_pool(name="squares", bufs=3))
        terms_pool = ctx.enter_context(tc.tile_pool(name="terms", bufs=2))
        stage_pool = ctx.enter_context(tc.tile_pool(name="stage", bufs=3))
        flip_psum = ctx.enter_context(tc.psum_pool(name="flip", bufs=4))
        acc_psum = ctx.enter_context(tc.psum_pool(name="acc", bufs=4))
        ctx.enter_context(tc.manual_schedule())

        gains_row = const.tile([P, 2 * D], BF16, name="gains_row")
        nc.vector.memset(gains_row[:], 0.0)
        nc.sync.dma_start(out=gains_row[0:1, 0:D], in_=q_norm_w.rearrange("(o d) -> o d", o=1))
        nc.sync.dma_start(out=gains_row[0:1, D : 2 * D], in_=k_norm_w.rearrange("(o d) -> o d", o=1))
        cos_sb = const.tile([P, TOKEN_TILES, D], BF16, name="cos_sb")
        sin_sb = const.tile([P, TOKEN_TILES, D], BF16, name="sin_sb")
        nc.sync.dma_start(
            out=cos_sb[:], in_=cos.flatten_outer_dims().rearrange("(p t) d -> p t d", t=TOKEN_TILES)
        )
        nc.sync.dma_start(
            out=sin_sb[:], in_=sin.flatten_outer_dims().rearrange("(p t) d -> p t d", t=TOKEN_TILES)
        )

        x_rows = hidden_states.flatten_outer_dims().rearrange("(p t) k -> p t k", t=TOKEN_TILES)
        unit_rows = [x_rows[:, i * UNIT_TILES : (i + 1) * UNIT_TILES, :] for i in range(X_UNITS)]
        for weight, units in ((Wq, Q_UNITS), (Wk, K_UNITS), (Wv, V_UNITS)):
            for i in range(units):
                rows = weight[i * UNIT_ROWS : (i + 1) * UNIT_ROWS, :]
                unit_rows.append(rows.rearrange("(r p) k -> p r k", p=P))

        raw = {}

        def load(unit):
            raw[unit] = raw_pool.tile([P, UNIT_TILES, HID], BF16, name="raw%d" % unit)
            nc.sync.dma_start(out=raw[unit][:], in_=unit_rows[unit])

        for unit in range(LOADS_AHEAD):
            load(unit)

        ident = const.tile([P, P], F32, name="ident")
        make_identity(nc, ident[:])
        ones = const.tile([P, P], BF16, name="ones")
        nc.vector.memset(ones[:], 1.0)
        eps_col = const.tile([P, 1], F32, name="eps_col")
        nc.vector.memset(eps_col[:], EPS)
        table_warm = const.tile([P, 1], F32, name="table_warm")
        nc.scalar.activation(out=table_warm[:], in_=eps_col[:], func=ACT.Abs_reciprocal_sqrt)

        gains_ps = flip_psum.tile([P, 2 * D], F32, tag="flip", name="gains_ps")
        nc.tensor.matmul(out=gains_ps[:], lhsT=ones[:], rhs=gains_row[:], start=True, stop=True)
        gains = const.tile([P, 2 * D], F32, name="gains")
        minus_gains = const.tile([P, 2 * D], F32, name="minus_gains")
        nc.scalar.copy(out=gains[:], in_=gains_ps[:])
        nc.scalar.mul(out=minus_gains[:], in_=gains_ps[:], mul=-1.0)

        rope = []
        for which in range(2):
            w_lo = slice(which * D, which * D + HALF)
            w_hi = slice(which * D + HALF, (which + 1) * D)
            table = const.tile([P, TOKEN_TILES, 2, D], F32, name="rope%d" % which)
            for row, columns, angles, gain in (
                (0, slice(0, HALF), cos_sb[:, :, 0:HALF], gains[:, w_lo]),
                (0, slice(HALF, D), sin_sb[:, :, 0:HALF], minus_gains[:, w_hi]),
                (1, slice(0, HALF), sin_sb[:, :, HALF:D], gains[:, w_lo]),
                (1, slice(HALF, D), cos_sb[:, :, HALF:D], gains[:, w_hi]),
            ):
                nc.gpsimd.tensor_tensor(
                    out=table[:, :, row, columns],
                    in0=angles,
                    in1=gain.unsqueeze(1).to_broadcast([P, TOKEN_TILES, HALF]),
                    op=ALU.mult,
                )
            rope.append(table)

        unit_out = []
        for out, units in ((out_0, Q_UNITS), (out_1, K_UNITS), (out_2, V_UNITS)):
            heads = out.rearrange("o h (p t) d -> p (o h) (t d)", t=TOKEN_TILES)
            for i in range(units):
                unit_out.append(heads[:, i * UNIT_TILES : (i + 1) * UNIT_TILES, :])

        banks = {}
        grouped = {}
        codes = {}
        scales = {}
        accs = {}
        sum_sq = {}
        inv_rms = {}
        terms = {}
        stages = {}

        def transposes(unit):
            words = raw[unit][:].bitcast(F32)
            for g in range(PASSES):
                bank = flip_psum.tile([P, 2, UNIT_ROWS], F32, tag="flip", name="bank")
                for r in range(UNIT_TILES):
                    for u in range(2):
                        first = g * PASS_WORDS + u * P
                        nc.tensor.transpose(
                            bank[:, u, r * P : (r + 1) * P], words[:, r, first : first + P], ident[:]
                        )
                banks[(unit, g)] = bank

        def copy_out(unit, g):
            pair, i = divmod(g, 2)
            if i == 0:
                grouped[(unit, pair)] = grouped_pool.tile(
                    [P, 2 * 4 * UNIT_ROWS], BF16, align_bytes=64, name="grouped"
                )
            grouped_words = grouped[(unit, pair)][:].bitcast(F32)
            engine_copy = nc.vector.tensor_copy if (unit <= LAG and i == 1) else nc.scalar.copy
            engine_copy(
                out=grouped_words[:, i * 2 * UNIT_ROWS : (i + 1) * 2 * UNIT_ROWS].rearrange(
                    "p (c u) -> p c u", u=2
                ),
                in_=banks[(unit, g)][:].rearrange("p u c -> p c u"),
            )

        def quantise(unit, pair):
            if pair == 0:
                pool = const if unit < X_UNITS else words_pool
                codes[unit] = pool.tile(
                    [P, PASSES * UNIT_ROWS], U32, align_bytes=64, name="codes%d" % min(unit, X_UNITS)
                )
                scales[unit] = pool.tile(
                    [P, PASSES * UNIT_ROWS], U8, align_bytes=64, name="scales%d" % min(unit, X_UNITS)
                )
            columns = slice(pair * 2 * UNIT_ROWS, (pair + 1) * 2 * UNIT_ROWS)
            nc.vector.quantize_mx(
                out=codes[unit][:, columns].bitcast(FP8X4),
                scales=scales[unit][:, columns],
                in_=grouped[(unit, pair)][:],
            )

        def matmuls(m):
            w = m + X_UNITS
            for x_unit in range(X_UNITS):
                acc = acc_psum.tile([P, UNIT_TILES, UNIT_ROWS], F32, tag="acc", name="acc")
                for i in range(UNIT_TILES):
                    for g in range(PASSES):
                        tokens = slice(g * UNIT_ROWS + i * P, g * UNIT_ROWS + (i + 1) * P)
                        features = slice(g * UNIT_ROWS, (g + 1) * UNIT_ROWS)
                        nc.tensor.matmul_mx(
                            out=acc[:, i, :],
                            lhsT=codes[x_unit][:, tokens].bitcast(FP8X4),
                            lhsT_scale=scales[x_unit][:, tokens],
                            rhs=codes[w][:, features].bitcast(FP8X4),
                            rhs_scale=scales[w][:, features],
                            start=(g == 0),
                            stop=(g == PASSES - 1),
                        )
                accs[(m, x_unit)] = acc

        def sum_squares(m, x_unit):
            acc = accs[(m, x_unit)]
            sum_sq[(m, x_unit)] = small.tile([P, UNIT_TILES * UNIT_TILES], F32, name="sum_sq")
            squares = squares_pool.tile([P, UNIT_TILES, UNIT_ROWS], F32, name="squares")
            for i in range(UNIT_TILES):
                for h in range(UNIT_TILES):
                    column = i * UNIT_TILES + h
                    nc.scalar.activation(
                        out=squares[:, i, h * D : (h + 1) * D],
                        in_=acc[:, i, h * D : (h + 1) * D],
                        func=ACT.Square,
                        accum_out=sum_sq[(m, x_unit)][:, column : column + 1],
                    )

        def inverse_rms(m, x_unit):
            inv_rms[(m, x_unit)] = small.tile([P, UNIT_TILES * UNIT_TILES], F32, name="inv_rms")
            nc.scalar.activation(
                out=inv_rms[(m, x_unit)][:],
                in_=sum_sq[(m, x_unit)][:],
                func=ACT.Abs_reciprocal_sqrt,
                bias=eps_col[:],
                scale=1.0 / D,
            )

        def scale_bank(m, x_unit):
            acc = accs[(m, x_unit)]
            inv = inv_rms[(m, x_unit)]
            if x_unit == 0:
                stages[m] = stage_pool.tile([P, UNIT_TILES, TOKEN_TILES, D], F32, name="stage")
            if m >= Q_UNITS + K_UNITS:
                tiles = slice(x_unit * UNIT_TILES, (x_unit + 1) * UNIT_TILES)
                nc.vector.tensor_tensor(
                    out=stages[m][:, :, tiles, :],
                    in0=acc[:].rearrange("p i (h d) -> p h i d", d=D),
                    in1=inv[:]
                    .rearrange("p (i h) -> p h i", h=UNIT_TILES)
                    .unsqueeze(3)
                    .to_broadcast([P, UNIT_TILES, UNIT_TILES, D]),
                    op=ALU.mult,
                )
                nc.sync.dma_start(
                    out=unit_out[m][:, :, x_unit * UNIT_ROWS : (x_unit + 1) * UNIT_ROWS],
                    in_=stages[m][:, :, tiles, :].rearrange("p h i d -> p h (i d)"),
                )
                return
            if x_unit == 0:
                terms[m] = terms_pool.tile([P, UNIT_TILES, TOKEN_TILES, 2, D], F32, name="terms")
            table = rope[0] if m < Q_UNITS else rope[1]
            for i in range(UNIT_TILES):
                t = x_unit * UNIT_TILES + i
                for h in range(UNIT_TILES):
                    column = i * UNIT_TILES + h
                    nc.vector.scalar_tensor_tensor(
                        out=terms[m][:, h, t, :, :],
                        in0=acc[:, i, h * D : (h + 1) * D].unsqueeze(1).to_broadcast([P, 2, D]),
                        scalar=inv[:, column : column + 1],
                        in1=table[:, t, :, :],
                        op0=ALU.mult,
                        op1=ALU.mult,
                    )

        def add_terms(m):
            pairs = terms[m][:].rearrange("p h t r (c j) -> p (h t r) c j", j=HALF)
            nc.gpsimd.tensor_tensor(
                out=stages[m][:].rearrange("p h t (r j) -> p (h t r) j", j=HALF),
                in0=pairs[:, :, 0, :],
                in1=pairs[:, :, 1, :],
                op=ALU.add,
            )

        def store(m):
            nc.sync.dma_start(out=unit_out[m], in_=stages[m][:].rearrange("p h t d -> p h (t d)"))

        for s in range(W_UNITS + LAG + 1):
            m = s - LAG
            prepare = s < UNITS
            multiply = 0 <= m < W_UNITS
            finish = 0 <= m - 1 < W_UNITS
            if s + LOADS_AHEAD < UNITS:
                load(s + LOADS_AHEAD)
            if prepare:
                transposes(s)
            if multiply:
                matmuls(m)
            if finish:
                sum_squares(m - 1, 1)
                inverse_rms(m - 1, 0)
            if prepare:
                copy_out(s, 0)
            if finish:
                inverse_rms(m - 1, 1)
            if prepare:
                for g in range(1, PASSES):
                    copy_out(s, g)
            if multiply:
                sum_squares(m, 0)
            if finish:
                scale_bank(m - 1, 0)
                scale_bank(m - 1, 1)
                if m - 1 < Q_UNITS + K_UNITS:
                    add_terms(m - 1)
            if 0 <= m - 2 < Q_UNITS + K_UNITS:
                store(m - 2)
            if prepare:
                quantise(s, 0)
                quantise(s, 1)
